import numpy as np
import ml_dtypes


def mxq(x, axis, fmt="e4m3"):
    dtype, down = {"e4m3": (ml_dtypes.float8_e4m3fn, 7), "e5m2": (ml_dtypes.float8_e5m2, 14)}[fmt]
    v = np.moveaxis(np.asarray(x, np.float32).astype(ml_dtypes.bfloat16).astype(np.float64), axis, -1)
    blocks = v.reshape(v.shape[:-1] + (-1, 32))
    amax = np.abs(blocks).max(-1, keepdims=True)
    byte = np.maximum(np.where(amax > 0, np.frexp(amax)[1] - 1 + 127, 0) - down, 1)
    scale = np.exp2(byte - 127.0)
    codes = (blocks / scale).astype(np.float32).astype(dtype).astype(np.float64)
    return np.moveaxis((codes * scale).reshape(v.shape), -1, axis)


WIDE = False


def mx_kscale(k):
    if not WIDE:
        return np.ones(k)
    levels = np.array([10, -10, 5, -5, 0])
    a = np.random.permutation(np.resize(levels, k // 512 * 4)).reshape(k // 512, 4)
    idx = np.arange(k)
    return np.exp2(a[idx // 512, idx % 128 // 32])


BF16 = ml_dtypes.bfloat16


def bf(x):
    return np.asarray(x, np.float32).astype(BF16)


def f64(x):
    return np.asarray(x).astype(np.float64)


E2M1 = np.array([0.0, 0.5, 1.0, 1.5, 2.0, 3.0, 4.0, 6.0, -0.0, -0.5, -1.0, -1.5, -2.0, -3.0, -4.0, -6.0])


def pack_weight(w, fmt):
    k, n = w.shape
    w = f64(bf(w)).reshape(k // 32, 32, n)
    amax = np.abs(w).max(1)
    if fmt == "e4m3":
        byte = np.frexp(amax)[1] - 1 + 127 - 7
    else:
        mant, ex = np.frexp(amax / 6.0)
        byte = np.where(mant > 0.5, ex, ex - 1) + 127
    byte = np.clip(np.where(amax > 0, byte, 1), 1, 254)
    scaled = (w * np.exp2(127.0 - byte)[:, None, :]).reshape(k, n).astype(np.float32)
    by_word = np.ascontiguousarray(scaled.reshape(k // 512, 128, 4, n).transpose(0, 1, 3, 2))
    if fmt == "e4m3":
        words = by_word.astype(ml_dtypes.float8_e4m3fn).view(np.uint8)
    else:
        c = by_word.astype(ml_dtypes.float4_e2m1fn).view(np.uint8) & 0xF
        words = c[..., 0::2] | (c[..., 1::2] << 4)
    return np.ascontiguousarray(words), np.ascontiguousarray(byte.astype(np.uint8).reshape(k // 512, 16, n))


def unpack_weight(words, scales, fmt):
    g, p, n, _ = words.shape
    if fmt == "e4m3":
        vals = np.ascontiguousarray(words).view(ml_dtypes.float8_e4m3fn).astype(np.float64)
    else:
        nib = np.empty((g, p, n, 4), np.uint8)
        nib[..., 0::2] = words & 0xF
        nib[..., 1::2] = words >> 4
        vals = E2M1[nib]
    vals = vals * np.repeat(np.exp2(scales.astype(np.float64) - 127.0), 8, axis=1)[..., None]
    return vals.transpose(0, 1, 3, 2).reshape(g * 512, n)

def pack4(w):
    words, scales = pack_weight(w, "e2m1")
    return words.reshape(words.shape[0], 128, -1), scales


def unpack4(words, scales):
    return unpack_weight(words.reshape(words.shape[0], 128, -1, 2), scales, "e2m1")


B, I, H, P = 512, 1024, 1024, 1024
CLOCKS = (0.5, 0.8, 0.95, 0.999)
TWO_PI = 2.0 * np.pi


def sigmoid(v):
    return 1.0 / (1.0 + np.exp(-v))


def setup_inputs():
    s = mx_kscale(I)
    x = bf(np.random.standard_normal((B, I)) * s)
    h_state = bf(np.random.standard_normal((B, H)))
    local_angle = bf(np.random.uniform(0.0, TWO_PI, (B, H)))
    persistence = bf(np.repeat(np.asarray(CLOCKS), H // len(CLOCKS)))
    ih_words, ih_scales = pack4(np.random.standard_normal((I, 3 * H)) * 0.7 / np.sqrt(I) / s[:, None])
    hh_words, hh_scales = pack4(np.random.standard_normal((H, 3 * H)) * 0.7 / np.sqrt(H))
    bias = bf(np.random.standard_normal(3 * H) * 0.3)
    return {
        "x": x,
        "h_state": h_state,
        "local_angle": local_angle,
        "persistence": persistence,
        "weight_ih_words": ih_words,
        "weight_ih_scales": ih_scales,
        "weight_hh_words": hh_words,
        "weight_hh_scales": hh_scales,
        "bias": bias,
    }


def reference(x, h_state, local_angle, persistence, weight_ih_words, weight_ih_scales, weight_hh_words, weight_hh_scales, bias):
    h = f64(h_state)
    gates = ((mxq(f64(x), 1, "e4m3") @ unpack4(weight_ih_words, weight_ih_scales))
             + (mxq(h, 1, "e4m3") @ unpack4(weight_hh_words, weight_hh_scales)) + f64(bias))
    r_gate, z_gate, n_gate = np.split(gates, 3, axis=-1)
    r = sigmoid(r_gate)
    z = sigmoid(z_gate)
    n = np.tanh(r * n_gate)
    phi_shift = z * TWO_PI
    raw_angle = f64(local_angle) * f64(persistence) + phi_shift
    h_blend = (1.0 - z) * h + z * n
    return (h_blend, raw_angle)

@@ -1,0 +1,249 @@
+import math
+from contextlib import ExitStack
+
+import concourse.mybir as mybir
+from concourse.masks import make_identity
+
+F32 = mybir.dt.float32
+BF16 = mybir.dt.bfloat16
+I32 = mybir.dt.int32
+U32 = mybir.dt.uint32
+U8 = mybir.dt.uint8
+FP8X4 = mybir.dt.float8_e4m3fn_x4
+FP4X4 = mybir.dt.float4_e2m1fn_x4
+ACT = mybir.ActivationFunctionType
+ALU = mybir.AluOpType
+
+P = 128
+BATCH = 512
+K = 1024
+HIDDEN = 1024
+GATES = 3
+K_PASS = 4 * P
+PASSES = K // K_PASS
+ROW_TILES = BATCH // P
+BLOCKS = HIDDEN // P
+W_CHUNKS = 4
+
+FLOPS = 2 * BATCH * (2 * K) * (GATES * HIDDEN)
+
+
+def tile_yarnixcellv4_pa_kernel(
+    tc,
+    x,
+    h_state,
+    local_angle,
+    persistence,
+    weight_ih_words,
+    weight_ih_scales,
+    weight_hh_words,
+    weight_hh_scales,
+    bias,
+    out_0,
+    out_1,
+):
+    nc = tc.nc
+    with ExitStack() as ctx:
+        keep = ctx.enter_context(tc.tile_pool(name="keep", bufs=1))
+        work = ctx.enter_context(tc.tile_pool(name="work", bufs=2))
+        gate_banks = ctx.enter_context(tc.psum_pool(name="gate_banks", bufs=6))
+        back_banks = ctx.enter_context(tc.psum_pool(name="back_banks", bufs=1))
+
+        ident_f32 = keep.tile([P, P], F32)
+        make_identity(nc, ident_f32[:])
+        ident_bf16 = keep.tile([P, P], BF16)
+        make_identity(nc, ident_bf16[:])
+        ones_bf16 = keep.tile([P, P], BF16)
+        nc.vector.memset(ones_bf16[:], 1.0)
+
+        warm = keep.tile([P, 1], F32)
+        nc.vector.memset(warm[:], 0.0)
+        nc.scalar.activation(out=warm[:], in_=warm[:], func=ACT.Sigmoid)
+
+        bias_rows = keep.tile([P, P], BF16)
+        nc.vector.memset(bias_rows[:], 0.0)
+        nc.scalar.dma_start(
+            out=bias_rows[0 : GATES * BLOCKS, :], in_=bias.rearrange("(i c) -> i c", c=P)
+        )
+        persist_row = keep.tile([P, HIDDEN], BF16)
+        nc.vector.memset(persist_row[:], 0.0)
+        nc.scalar.dma_start(
+            out=persist_row[0:1, :], in_=persistence.rearrange("(o n) -> o n", o=1)
+        )
+
+        w_planes = keep.tile([P, 2, PASSES, GATES * HIDDEN], U8, align_bytes=64)
+        nc.vector.memset(w_planes[:].bitcast(I32), 0)
+
+        x_sb = keep.tile([P, ROW_TILES, K], BF16)
+        h_sb = keep.tile([P, ROW_TILES, K], BF16)
+        angle_sb = keep.tile([P, ROW_TILES, HIDDEN], BF16)
+        for dram, sb in ((x, x_sb), (h_state, h_sb)):
+            rows = dram.rearrange("(m p) k -> p m k", p=P)
+            for m in range(ROW_TILES):
+                nc.sync.dma_start(out=sb[:, m, :], in_=rows[:, m, :])
+
+        for a, scales in enumerate((weight_ih_scales, weight_hh_scales)):
+            by_row = scales.rearrange("g (qh ql r) n -> ql r qh g n", ql=2, r=4)
+            for ql in range(2):
+                for r in range(4):
+                    nc.sync.dma_start(
+                        out=w_planes[32 * ql + r : P : 64, a, :, :].bitcast(I32),
+                        in_=by_row[ql, r].bitcast(I32),
+                    )
+
+        w_words = keep.tile([P, 2, PASSES, 2 * GATES * HIDDEN], U8, align_bytes=64)
+
+        def load_weight_chunk(chunk):
+            for a, words in enumerate((weight_ih_words, weight_hh_words)):
+                for g in range(PASSES):
+                    nc.sync.dma_start(
+                        out=w_words[:, a, g, :]
+                        .bitcast(I32)
+                        .rearrange("p (gate q c) -> p gate q c", gate=GATES, q=W_CHUNKS)[
+                            :, :, chunk, :
+                        ],
+                        in_=words[g]
+                        .bitcast(I32)
+                        .rearrange("p (gate q c) -> p gate q c", gate=GATES, q=W_CHUNKS)[
+                            :, :, chunk, :
+                        ],
+                    )
+
+        load_weight_chunk(0)
+        load_weight_chunk(1)
+        nc.sync.dma_start(
+            out=angle_sb[:], in_=local_angle.rearrange("(m p) j -> p m j", p=P)
+        )
+        load_weight_chunk(2)
+        load_weight_chunk(3)
+
+        act_codes = keep.tile([P, 2, PASSES, BATCH], U32, align_bytes=64)
+        act_planes = keep.tile([P, 2, PASSES, BATCH], U8, align_bytes=64)
+        for a, sb in enumerate((x_sb, h_sb)):
+            grouped = keep.tile(
+                [P, PASSES, 4 * BATCH], BF16, align_bytes=64, name="grouped%d" % a
+            )
+            grouped_words = grouped[:].bitcast(F32).rearrange("p g (b u) -> p g b u", u=2)
+            for m in range(ROW_TILES):
+                row_words = sb[:, m, :].bitcast(F32)
+                flipped = gate_banks.tile([P, PASSES, 2, P], F32, tag="bank")
+                for g in range(PASSES):
+                    for u in range(2):
+                        nc.tensor.transpose(
+                            flipped[:, g, u, :],
+                            row_words[:, 256 * g + u : 256 * (g + 1) : 2],
+                            ident_f32[:],
+                        )
+                copy_out = nc.vector.tensor_copy if m % 2 == 0 else nc.scalar.copy
+                copy_out(
+                    out=grouped_words[:, :, m * P : (m + 1) * P, :],
+                    in_=flipped[:].rearrange("p g u b -> p g b u"),
+                )
+            for g in range(PASSES):
+                nc.vector.quantize_mx(
+                    out=act_codes[:, a, g, :].bitcast(FP8X4),
+                    scales=act_planes[:, a, g, :],
+                    in_=grouped[:, g, :],
+                )
+
+        bias_flipped = gate_banks.tile([P, P], BF16, tag="bank")
+        nc.tensor.transpose(bias_flipped[:], bias_rows[:], ident_bf16[:])
+        bias_col = keep.tile([P, GATES * BLOCKS], F32)
+        nc.vector.tensor_copy(out=bias_col[:], in_=bias_flipped[:, 0 : GATES * BLOCKS])
+
+        persist_all = keep.tile([P, HIDDEN], BF16)
+        for s in range(HIDDEN // BATCH):
+            cols = slice(s * BATCH, (s + 1) * BATCH)
+            spread = gate_banks.tile([P, BATCH], F32, tag="bank")
+            nc.tensor.matmul(
+                out=spread[:], lhsT=ones_bf16[:], rhs=persist_row[:, cols], start=True, stop=True
+            )
+            nc.scalar.copy(out=persist_all[:, cols], in_=spread[:])
+
+        def gates_of_block(c):
+            r_ps = gate_banks.tile([P, BATCH], F32, tag="bank")
+            z_ps = gate_banks.tile([P, BATCH], F32, tag="bank")
+            n_ps = gate_banks.tile([P, BATCH], F32, tag="bank")
+            steps = 2 * PASSES
+            for step in range(steps):
+                a, g = divmod(step, PASSES)
+                for gate, bank in enumerate((r_ps, z_ps, n_ps)):
+                    col = gate * HIDDEN + c * P
+                    nc.tensor.matmul_mx(
+                        out=bank[:],
+                        lhsT=w_words[:, a, g, 2 * col : 2 * (col + P)].bitcast(FP4X4),
+                        lhsT_scale=w_planes[:, a, g, col : col + P],
+                        rhs=act_codes[:, a, g, :].bitcast(FP8X4),
+                        rhs_scale=act_planes[:, a, g, :],
+                        start=(step == 0),
+                        stop=(step == steps - 1),
+                    )
+            r_sb = work.tile([P, BATCH], F32)
+            nc.scalar.activation(
+                out=r_sb[:], in_=r_ps[:], func=ACT.Sigmoid, bias=bias_col[:, c : c + 1]
+            )
+            z_sb = work.tile([P, BATCH], F32)
+            nc.scalar.activation(
+                out=z_sb[:],
+                in_=z_ps[:],
+                func=ACT.Sigmoid,
+                bias=bias_col[:, BLOCKS + c : BLOCKS + c + 1],
+            )
+            rn_sb = work.tile([P, BATCH], F32)
+            nc.vector.scalar_tensor_tensor(
+                out=rn_sb[:],
+                in0=n_ps[:],
+                scalar=bias_col[:, 2 * BLOCKS + c : 2 * BLOCKS + c + 1],
+                in1=r_sb[:],
+                op0=ALU.add,
+                op1=ALU.mult,
+            )
+            n_sb = work.tile([P, BATCH], F32)
+            nc.scalar.activation(out=n_sb[:], in_=rn_sb[:], func=ACT.Tanh)
+            return z_sb, n_sb
+
+        def outputs_of_block(c, z_sb, n_sb):
+            cols = slice(c * P, (c + 1) * P)
+            decayed = work.tile([P, ROW_TILES, P], F32)
+            nc.gpsimd.tensor_tensor(
+                out=decayed[:],
+                in0=angle_sb[:, :, cols],
+                in1=persist_all[:, cols].unsqueeze(1).to_broadcast([P, ROW_TILES, P]),
+                op=ALU.mult,
+            )
+            n_back = back_banks.tile([P, ROW_TILES, P], F32)
+            z_back = back_banks.tile([P, ROW_TILES, P], F32)
+            for src, back in ((n_sb, n_back), (z_sb, z_back)):
+                for m in range(ROW_TILES):
+                    nc.tensor.transpose(back[:, m, :], src[:, m * P : (m + 1) * P], ident_f32[:])
+            diff = work.tile([P, ROW_TILES, P], F32)
+            nc.vector.tensor_tensor(
+                out=diff[:], in0=n_back[:], in1=h_sb[:, :, cols], op=ALU.subtract
+            )
+            step_sb = work.tile([P, ROW_TILES, P], F32)
+            nc.vector.tensor_tensor(out=step_sb[:], in0=diff[:], in1=z_back[:], op=ALU.mult)
+            blend = work.tile([P, ROW_TILES, P], F32)
+            nc.vector.tensor_tensor(out=blend[:], in0=step_sb[:], in1=h_sb[:, :, cols], op=ALU.add)
+            nc.sync.dma_start(
+                out=out_0.rearrange("(m p) j -> p m j", p=P)[:, :, cols], in_=blend[:]
+            )
+            angle_out = work.tile([P, ROW_TILES, P], F32)
+            nc.vector.scalar_tensor_tensor(
+                out=angle_out[:],
+                in0=z_back[:],
+                scalar=2.0 * math.pi,
+                in1=decayed[:],
+                op0=ALU.mult,
+                op1=ALU.add,
+            )
+            nc.sync.dma_start(
+                out=out_1.rearrange("(m p) j -> p m j", p=P)[:, :, cols], in_=angle_out[:]
+            )
+
+        waiting = None
+        for c in range(BLOCKS):
+            fresh = gates_of_block(c)
+            if waiting is not None:
+                outputs_of_block(c - 1, waiting[0], waiting[1])
+            waiting = fresh
+        outputs_of_block(BLOCKS - 1, waiting[0], waiting[1])

@@ -48,6 +48,7 @@ def tile_yarnixcellv4_pa_kernel(
         work = ctx.enter_context(tc.tile_pool(name="work", bufs=2))
         gate_banks = ctx.enter_context(tc.psum_pool(name="gate_banks", bufs=6))
         back_banks = ctx.enter_context(tc.psum_pool(name="back_banks", bufs=1))
+        ctx.enter_context(tc.manual_schedule())
 
         ident_f32 = keep.tile([P, P], F32)
         make_identity(nc, ident_f32[:])

@@ -19,6 +19,7 @@ BATCH = 512
 K = 1024
 HIDDEN = 1024
 GATES = 3
+R, Z, N = 0, 1, 2
 K_PASS = 4 * P
 PASSES = K // K_PASS
 ROW_TILES = BATCH // P
@@ -50,6 +51,9 @@ def tile_yarnixcellv4_pa_kernel(
         back_banks = ctx.enter_context(tc.psum_pool(name="back_banks", bufs=1))
         ctx.enter_context(tc.manual_schedule())
 
+        w_planes = keep.tile([P, 2, PASSES, GATES * HIDDEN], U8, align_bytes=64)
+        nc.vector.memset(w_planes[:].bitcast(I32), 0)
+
         ident_f32 = keep.tile([P, P], F32)
         make_identity(nc, ident_f32[:])
         ident_bf16 = keep.tile([P, P], BF16)
@@ -63,34 +67,29 @@ def tile_yarnixcellv4_pa_kernel(
 
         bias_rows = keep.tile([P, P], BF16)
         nc.vector.memset(bias_rows[:], 0.0)
-        nc.scalar.dma_start(
+        nc.gpsimd.dma_start(
             out=bias_rows[0 : GATES * BLOCKS, :], in_=bias.rearrange("(i c) -> i c", c=P)
         )
         persist_row = keep.tile([P, HIDDEN], BF16)
         nc.vector.memset(persist_row[:], 0.0)
-        nc.scalar.dma_start(
+        nc.gpsimd.dma_start(
             out=persist_row[0:1, :], in_=persistence.rearrange("(o n) -> o n", o=1)
         )
-
-        w_planes = keep.tile([P, 2, PASSES, GATES * HIDDEN], U8, align_bytes=64)
-        nc.vector.memset(w_planes[:].bitcast(I32), 0)
 
         x_sb = keep.tile([P, ROW_TILES, K], BF16)
         h_sb = keep.tile([P, ROW_TILES, K], BF16)
         angle_sb = keep.tile([P, ROW_TILES, HIDDEN], BF16)
         for dram, sb in ((x, x_sb), (h_state, h_sb)):
             rows = dram.rearrange("(m p) k -> p m k", p=P)
-            for m in range(ROW_TILES):
-                nc.sync.dma_start(out=sb[:, m, :], in_=rows[:, m, :])
+            for m in range(0, ROW_TILES, 2):
+                nc.sync.dma_start(out=sb[:, m : m + 2, :], in_=rows[:, m : m + 2, :])
 
         for a, scales in enumerate((weight_ih_scales, weight_hh_scales)):
-            by_row = scales.rearrange("g (qh ql r) n -> ql r qh g n", ql=2, r=4)
-            for ql in range(2):
-                for r in range(4):
-                    nc.sync.dma_start(
-                        out=w_planes[32 * ql + r : P : 64, a, :, :].bitcast(I32),
-                        in_=by_row[ql, r].bitcast(I32),
-                    )
+            by_row = scales.rearrange("g (quad r) n -> r quad g n", r=4)
+            for r in range(4):
+                nc.sync.dma_start(
+                    out=w_planes[r:P:32, a, :, :].bitcast(I32), in_=by_row[r].bitcast(I32)
+                )
 
         w_words = keep.tile([P, 2, PASSES, 2 * GATES * HIDDEN], U8, align_bytes=64)
 
@@ -161,47 +160,44 @@ def tile_yarnixcellv4_pa_kernel(
             )
             nc.scalar.copy(out=persist_all[:, cols], in_=spread[:])
 
-        def gates_of_block(c):
-            r_ps = gate_banks.tile([P, BATCH], F32, tag="bank")
-            z_ps = gate_banks.tile([P, BATCH], F32, tag="bank")
-            n_ps = gate_banks.tile([P, BATCH], F32, tag="bank")
-            steps = 2 * PASSES
-            for step in range(steps):
-                a, g = divmod(step, PASSES)
-                for gate, bank in enumerate((r_ps, z_ps, n_ps)):
-                    col = gate * HIDDEN + c * P
-                    nc.tensor.matmul_mx(
-                        out=bank[:],
-                        lhsT=w_words[:, a, g, 2 * col : 2 * (col + P)].bitcast(FP4X4),
-                        lhsT_scale=w_planes[:, a, g, col : col + P],
-                        rhs=act_codes[:, a, g, :].bitcast(FP8X4),
-                        rhs_scale=act_planes[:, a, g, :],
-                        start=(step == 0),
-                        stop=(step == steps - 1),
-                    )
+        STEPS = 2 * PASSES
+
+        def mx_pass(bank, gate, c, step):
+            a, g = divmod(step, PASSES)
+            col = gate * HIDDEN + c * P
+            nc.tensor.matmul_mx(
+                out=bank[:],
+                lhsT=w_words[:, a, g, 2 * col : 2 * (col + P)].bitcast(FP4X4),
+                lhsT_scale=w_planes[:, a, g, col : col + P],
+                rhs=act_codes[:, a, g, :].bitcast(FP8X4),
+                rhs_scale=act_planes[:, a, g, :],
+                start=(step == 0),
+                stop=(step == STEPS - 1),
+            )
+
+        def bias_of(gate, c):
+            return bias_col[:, gate * BLOCKS + c : gate * BLOCKS + c + 1]
+
+        def candidate(c, r_ps, n_ps):
             r_sb = work.tile([P, BATCH], F32)
-            nc.scalar.activation(
-                out=r_sb[:], in_=r_ps[:], func=ACT.Sigmoid, bias=bias_col[:, c : c + 1]
-            )
-            z_sb = work.tile([P, BATCH], F32)
-            nc.scalar.activation(
-                out=z_sb[:],
-                in_=z_ps[:],
-                func=ACT.Sigmoid,
-                bias=bias_col[:, BLOCKS + c : BLOCKS + c + 1],
-            )
+            nc.scalar.activation(out=r_sb[:], in_=r_ps[:], func=ACT.Sigmoid, bias=bias_of(R, c))
             rn_sb = work.tile([P, BATCH], F32)
             nc.vector.scalar_tensor_tensor(
                 out=rn_sb[:],
                 in0=n_ps[:],
-                scalar=bias_col[:, 2 * BLOCKS + c : 2 * BLOCKS + c + 1],
+                scalar=bias_of(N, c),
                 in1=r_sb[:],
                 op0=ALU.add,
                 op1=ALU.mult,
             )
             n_sb = work.tile([P, BATCH], F32)
             nc.scalar.activation(out=n_sb[:], in_=rn_sb[:], func=ACT.Tanh)
-            return z_sb, n_sb
+            return n_sb
+
+        def update(c, z_ps):
+            z_sb = work.tile([P, BATCH], F32)
+            nc.scalar.activation(out=z_sb[:], in_=z_ps[:], func=ACT.Sigmoid, bias=bias_of(Z, c))
+            return z_sb
 
         def outputs_of_block(c, z_sb, n_sb):
             cols = slice(c * P, (c + 1) * P)
@@ -241,10 +237,25 @@ def tile_yarnixcellv4_pa_kernel(
                 out=out_1.rearrange("(m p) j -> p m j", p=P)[:, :, cols], in_=angle_out[:]
             )
 
-        waiting = None
         for c in range(BLOCKS):
-            fresh = gates_of_block(c)
-            if waiting is not None:
-                outputs_of_block(c - 1, waiting[0], waiting[1])
-            waiting = fresh
-        outputs_of_block(BLOCKS - 1, waiting[0], waiting[1])
+            r_ps = gate_banks.tile([P, BATCH], F32, tag="bank")
+            n_ps = gate_banks.tile([P, BATCH], F32, tag="bank")
+            z_ps = gate_banks.tile([P, BATCH], F32, tag="bank")
+            if c == 0:
+                for step in range(STEPS):
+                    mx_pass(r_ps, R, c, step)
+                    mx_pass(n_ps, N, c, step)
+                    mx_pass(z_ps, Z, c, step)
+                n_sb = candidate(c, r_ps, n_ps)
+            else:
+                for step in range(STEPS):
+                    mx_pass(r_ps, R, c, step)
+                for step in range(STEPS):
+                    mx_pass(n_ps, N, c, step)
+                n_before, z_before = n_sb, z_sb
+                n_sb = candidate(c, r_ps, n_ps)
+                outputs_of_block(c - 1, z_before, n_before)
+                for step in range(STEPS):
+                    mx_pass(z_ps, Z, c, step)
+            z_sb = update(c, z_ps)
+        outputs_of_block(BLOCKS - 1, z_sb, n_sb)

@@ -25,6 +25,7 @@ PASSES = K // K_PASS
 ROW_TILES = BATCH // P
 BLOCKS = HIDDEN // P
 W_CHUNKS = 4
+CHUNK_BLOCKS = BLOCKS // W_CHUNKS
 
 FLOPS = 2 * BATCH * (2 * K) * (GATES * HIDDEN)
 
@@ -52,7 +53,57 @@ def tile_yarnixcellv4_pa_kernel(
         ctx.enter_context(tc.manual_schedule())
 
         w_planes = keep.tile([P, 2, PASSES, GATES * HIDDEN], U8, align_bytes=64)
-        nc.vector.memset(w_planes[:].bitcast(I32), 0)
+        for a in range(2):
+            nc.vector.memset(w_planes[:, a, :, :].bitcast(I32), 0)
+
+        def load_scales(a, scales):
+            by_row = scales.rearrange("g (quad r) n -> r quad g n", r=4)
+            for r in range(4):
+                nc.sync.dma_start(
+                    out=w_planes[r:P:32, a, :, :].bitcast(I32), in_=by_row[r].bitcast(I32)
+                )
+
+        chunk_bytes = 2 * CHUNK_BLOCKS * P
+        w_words = [
+            keep.tile(
+                [P, 2, PASSES, GATES, chunk_bytes], U8, align_bytes=64, name="w_words%d" % chunk
+            )
+            for chunk in range(W_CHUNKS)
+        ]
+
+        def load_words(chunk, a, words):
+            for g in range(PASSES):
+                nc.sync.dma_start(
+                    out=w_words[chunk][:, a, g, :, :].bitcast(I32),
+                    in_=words[g]
+                    .bitcast(I32)
+                    .rearrange("p (gate q c) -> p gate q c", gate=GATES, q=W_CHUNKS)[
+                        :, :, chunk, :
+                    ],
+                )
+
+        x_sb = keep.tile([P, ROW_TILES, K], BF16)
+        h_sb = keep.tile([P, ROW_TILES, K], BF16)
+        angle_sb = keep.tile([P, ROW_TILES, HIDDEN], BF16)
+
+        def load_rows(sb, dram):
+            rows = dram.rearrange("(m p) k -> p m k", p=P)
+            for m in range(0, ROW_TILES, 2):
+                nc.sync.dma_start(out=sb[:, m : m + 2, :], in_=rows[:, m : m + 2, :])
+
+        load_rows(x_sb, x)
+        load_scales(0, weight_ih_scales)
+        load_rows(h_sb, h_state)
+        load_words(0, 0, weight_ih_words)
+        load_scales(1, weight_hh_scales)
+        load_words(0, 1, weight_hh_words)
+        for chunk in range(1, W_CHUNKS):
+            load_words(chunk, 0, weight_ih_words)
+            load_words(chunk, 1, weight_hh_words)
+            if chunk == 1:
+                nc.sync.dma_start(
+                    out=angle_sb[:], in_=local_angle.rearrange("(m p) j -> p m j", p=P)
+                )
 
         ident_f32 = keep.tile([P, P], F32)
         make_identity(nc, ident_f32[:])
@@ -76,47 +127,6 @@ def tile_yarnixcellv4_pa_kernel(
             out=persist_row[0:1, :], in_=persistence.rearrange("(o n) -> o n", o=1)
         )
 
-        x_sb = keep.tile([P, ROW_TILES, K], BF16)
-        h_sb = keep.tile([P, ROW_TILES, K], BF16)
-        angle_sb = keep.tile([P, ROW_TILES, HIDDEN], BF16)
-        for dram, sb in ((x, x_sb), (h_state, h_sb)):
-            rows = dram.rearrange("(m p) k -> p m k", p=P)
-            for m in range(0, ROW_TILES, 2):
-                nc.sync.dma_start(out=sb[:, m : m + 2, :], in_=rows[:, m : m + 2, :])
-
-        for a, scales in enumerate((weight_ih_scales, weight_hh_scales)):
-            by_row = scales.rearrange("g (quad r) n -> r quad g n", r=4)
-            for r in range(4):
-                nc.sync.dma_start(
-                    out=w_planes[r:P:32, a, :, :].bitcast(I32), in_=by_row[r].bitcast(I32)
-                )
-
-        w_words = keep.tile([P, 2, PASSES, 2 * GATES * HIDDEN], U8, align_bytes=64)
-
-        def load_weight_chunk(chunk):
-            for a, words in enumerate((weight_ih_words, weight_hh_words)):
-                for g in range(PASSES):
-                    nc.sync.dma_start(
-                        out=w_words[:, a, g, :]
-                        .bitcast(I32)
-                        .rearrange("p (gate q c) -> p gate q c", gate=GATES, q=W_CHUNKS)[
-                            :, :, chunk, :
-                        ],
-                        in_=words[g]
-                        .bitcast(I32)
-                        .rearrange("p (gate q c) -> p gate q c", gate=GATES, q=W_CHUNKS)[
-                            :, :, chunk, :
-                        ],
-                    )
-
-        load_weight_chunk(0)
-        load_weight_chunk(1)
-        nc.sync.dma_start(
-            out=angle_sb[:], in_=local_angle.rearrange("(m p) j -> p m j", p=P)
-        )
-        load_weight_chunk(2)
-        load_weight_chunk(3)
-
         act_codes = keep.tile([P, 2, PASSES, BATCH], U32, align_bytes=64)
         act_planes = keep.tile([P, 2, PASSES, BATCH], U8, align_bytes=64)
         for a, sb in enumerate((x_sb, h_sb)):
@@ -124,21 +134,22 @@ def tile_yarnixcellv4_pa_kernel(
                 [P, PASSES, 4 * BATCH], BF16, align_bytes=64, name="grouped%d" % a
             )
             grouped_words = grouped[:].bitcast(F32).rearrange("p g (b u) -> p g b u", u=2)
-            for m in range(ROW_TILES):
-                row_words = sb[:, m, :].bitcast(F32)
-                flipped = gate_banks.tile([P, PASSES, 2, P], F32, tag="bank")
+            for m in range(0, ROW_TILES, 2):
                 for g in range(PASSES):
-                    for u in range(2):
-                        nc.tensor.transpose(
-                            flipped[:, g, u, :],
-                            row_words[:, 256 * g + u : 256 * (g + 1) : 2],
-                            ident_f32[:],
-                        )
-                copy_out = nc.vector.tensor_copy if m % 2 == 0 else nc.scalar.copy
-                copy_out(
-                    out=grouped_words[:, :, m * P : (m + 1) * P, :],
-                    in_=flipped[:].rearrange("p g u b -> p g b u"),
-                )
+                    flipped = gate_banks.tile([P, 2, 2, P], F32, tag="bank")
+                    for i in range(2):
+                        row_words = sb[:, m + i, :].bitcast(F32)
+                        for u in range(2):
+                            nc.tensor.transpose(
+                                flipped[:, u, i, :],
+                                row_words[:, 256 * g + u : 256 * (g + 1) : 2],
+                                ident_f32[:],
+                            )
+                    copy_out = nc.vector.tensor_copy if g == 0 else nc.scalar.copy
+                    copy_out(
+                        out=grouped_words[:, g, m * P : (m + 2) * P, :],
+                        in_=flipped[:].rearrange("p u i b -> p (i b) u"),
+                    )
             for g in range(PASSES):
                 nc.vector.quantize_mx(
                     out=act_codes[:, a, g, :].bitcast(FP8X4),
@@ -160,20 +171,28 @@ def tile_yarnixcellv4_pa_kernel(
             )
             nc.scalar.copy(out=persist_all[:, cols], in_=spread[:])
 
-        STEPS = 2 * PASSES
-
-        def mx_pass(bank, gate, c, step):
-            a, g = divmod(step, PASSES)
+        def mx_passes(bank, gate, c, a):
+            chunk, i = divmod(c, CHUNK_BLOCKS)
             col = gate * HIDDEN + c * P
-            nc.tensor.matmul_mx(
-                out=bank[:],
-                lhsT=w_words[:, a, g, 2 * col : 2 * (col + P)].bitcast(FP4X4),
-                lhsT_scale=w_planes[:, a, g, col : col + P],
-                rhs=act_codes[:, a, g, :].bitcast(FP8X4),
-                rhs_scale=act_planes[:, a, g, :],
-                start=(step == 0),
-                stop=(step == STEPS - 1),
-            )
+            for g in range(PASSES):
+                nc.tensor.matmul_mx(
+                    out=bank[:],
+                    lhsT=w_words[chunk][:, a, g, gate, 2 * P * i : 2 * P * (i + 1)].bitcast(FP4X4),
+                    lhsT_scale=w_planes[:, a, g, col : col + P],
+                    rhs=act_codes[:, a, g, :].bitcast(FP8X4),
+                    rhs_scale=act_planes[:, a, g, :],
+                    start=(a == 0 and g == 0),
+                    stop=(a == 1 and g == PASSES - 1),
+                )
+
+        def open_block(c):
+            r_ps = gate_banks.tile([P, BATCH], F32, tag="bank")
+            n_ps = gate_banks.tile([P, BATCH], F32, tag="bank")
+            z_ps = gate_banks.tile([P, BATCH], F32, tag="bank")
+            mx_passes(r_ps, R, c, 0)
+            mx_passes(n_ps, N, c, 0)
+            mx_passes(z_ps, Z, c, 0)
+            return r_ps, n_ps, z_ps
 
         def bias_of(gate, c):
             return bias_col[:, gate * BLOCKS + c : gate * BLOCKS + c + 1]
@@ -237,25 +256,18 @@ def tile_yarnixcellv4_pa_kernel(
                 out=out_1.rearrange("(m p) j -> p m j", p=P)[:, :, cols], in_=angle_out[:]
             )
 
+        banks = open_block(0)
+        finished = None
         for c in range(BLOCKS):
-            r_ps = gate_banks.tile([P, BATCH], F32, tag="bank")
-            n_ps = gate_banks.tile([P, BATCH], F32, tag="bank")
-            z_ps = gate_banks.tile([P, BATCH], F32, tag="bank")
-            if c == 0:
-                for step in range(STEPS):
-                    mx_pass(r_ps, R, c, step)
-                    mx_pass(n_ps, N, c, step)
-                    mx_pass(z_ps, Z, c, step)
-                n_sb = candidate(c, r_ps, n_ps)
-            else:
-                for step in range(STEPS):
-                    mx_pass(r_ps, R, c, step)
-                for step in range(STEPS):
-                    mx_pass(n_ps, N, c, step)
-                n_before, z_before = n_sb, z_sb
-                n_sb = candidate(c, r_ps, n_ps)
-                outputs_of_block(c - 1, z_before, n_before)
-                for step in range(STEPS):
-                    mx_pass(z_ps, Z, c, step)
+            r_ps, n_ps, z_ps = banks
+            mx_passes(r_ps, R, c, 1)
+            mx_passes(n_ps, N, c, 1)
+            n_sb = candidate(c, r_ps, n_ps)
+            if finished is not None:
+                outputs_of_block(c - 1, finished[0], finished[1])
+            mx_passes(z_ps, Z, c, 1)
             z_sb = update(c, z_ps)
-        outputs_of_block(BLOCKS - 1, z_sb, n_sb)
+            finished = (z_sb, n_sb)
+            if c + 1 < BLOCKS:
+                banks = open_block(c + 1)
+        outputs_of_block(BLOCKS - 1, finished[0], finished[1])

@@ -239,10 +239,7 @@ def tile_yarnixcellv4_pa_kernel(
             step_sb = work.tile([P, ROW_TILES, P], F32)
             nc.vector.tensor_tensor(out=step_sb[:], in0=diff[:], in1=z_back[:], op=ALU.mult)
             blend = work.tile([P, ROW_TILES, P], F32)
-            nc.vector.tensor_tensor(out=blend[:], in0=step_sb[:], in1=h_sb[:, :, cols], op=ALU.add)
-            nc.sync.dma_start(
-                out=out_0.rearrange("(m p) j -> p m j", p=P)[:, :, cols], in_=blend[:]
-            )
+            nc.gpsimd.tensor_tensor(out=blend[:], in0=step_sb[:], in1=h_sb[:, :, cols], op=ALU.add)
             angle_out = work.tile([P, ROW_TILES, P], F32)
             nc.vector.scalar_tensor_tensor(
                 out=angle_out[:],
@@ -255,11 +252,14 @@ def tile_yarnixcellv4_pa_kernel(
             nc.sync.dma_start(
                 out=out_1.rearrange("(m p) j -> p m j", p=P)[:, :, cols], in_=angle_out[:]
             )
+            nc.sync.dma_start(
+                out=out_0.rearrange("(m p) j -> p m j", p=P)[:, :, cols], in_=blend[:]
+            )
 
-        banks = open_block(0)
+        opened = [open_block(0), open_block(1)]
         finished = None
         for c in range(BLOCKS):
-            r_ps, n_ps, z_ps = banks
+            r_ps, n_ps, z_ps = opened[c]
             mx_passes(r_ps, R, c, 1)
             mx_passes(n_ps, N, c, 1)
             n_sb = candidate(c, r_ps, n_ps)
@@ -268,6 +268,6 @@ def tile_yarnixcellv4_pa_kernel(
             mx_passes(z_ps, Z, c, 1)
             z_sb = update(c, z_ps)
             finished = (z_sb, n_sb)
-            if c + 1 < BLOCKS:
-                banks = open_block(c + 1)
+            if len(opened) == c + 1 and c + 1 < BLOCKS:
+                opened.append(open_block(c + 1))
         outputs_of_block(BLOCKS - 1, finished[0], finished[1])

@@ -50,7 +50,6 @@ def tile_yarnixcellv4_pa_kernel(
         work = ctx.enter_context(tc.tile_pool(name="work", bufs=2))
         gate_banks = ctx.enter_context(tc.psum_pool(name="gate_banks", bufs=6))
         back_banks = ctx.enter_context(tc.psum_pool(name="back_banks", bufs=1))
-        ctx.enter_context(tc.manual_schedule())
 
         w_planes = keep.tile([P, 2, PASSES, GATES * HIDDEN], U8, align_bytes=64)
         for a in range(2):

@@ -190,7 +190,8 @@ def tile_yarnixcellv4_pa_kernel(
             z_ps = gate_banks.tile([P, BATCH], F32, tag="bank")
             mx_passes(r_ps, R, c, 0)
             mx_passes(n_ps, N, c, 0)
-            mx_passes(z_ps, Z, c, 0)
+            if c < BLOCKS - 1:
+                mx_passes(z_ps, Z, c, 0)
             return r_ps, n_ps, z_ps
 
         def bias_of(gate, c):
@@ -217,7 +218,7 @@ def tile_yarnixcellv4_pa_kernel(
             nc.scalar.activation(out=z_sb[:], in_=z_ps[:], func=ACT.Sigmoid, bias=bias_of(Z, c))
             return z_sb
 
-        def outputs_of_block(c, z_sb, n_sb):
+        def turn_back(c, z_sb, n_sb):
             cols = slice(c * P, (c + 1) * P)
             decayed = work.tile([P, ROW_TILES, P], F32)
             nc.gpsimd.tensor_tensor(
@@ -231,14 +232,14 @@ def tile_yarnixcellv4_pa_kernel(
             for src, back in ((n_sb, n_back), (z_sb, z_back)):
                 for m in range(ROW_TILES):
                     nc.tensor.transpose(back[:, m, :], src[:, m * P : (m + 1) * P], ident_f32[:])
+            return decayed, n_back, z_back
+
+        def outputs_of_block(c, decayed, n_back, z_back):
+            cols = slice(c * P, (c + 1) * P)
             diff = work.tile([P, ROW_TILES, P], F32)
             nc.vector.tensor_tensor(
                 out=diff[:], in0=n_back[:], in1=h_sb[:, :, cols], op=ALU.subtract
             )
-            step_sb = work.tile([P, ROW_TILES, P], F32)
-            nc.vector.tensor_tensor(out=step_sb[:], in0=diff[:], in1=z_back[:], op=ALU.mult)
-            blend = work.tile([P, ROW_TILES, P], F32)
-            nc.gpsimd.tensor_tensor(out=blend[:], in0=step_sb[:], in1=h_sb[:, :, cols], op=ALU.add)
             angle_out = work.tile([P, ROW_TILES, P], F32)
             nc.vector.scalar_tensor_tensor(
                 out=angle_out[:],
@@ -248,6 +249,10 @@ def tile_yarnixcellv4_pa_kernel(
                 op0=ALU.mult,
                 op1=ALU.add,
             )
+            step_sb = work.tile([P, ROW_TILES, P], F32)
+            nc.vector.tensor_tensor(out=step_sb[:], in0=diff[:], in1=z_back[:], op=ALU.mult)
+            blend = work.tile([P, ROW_TILES, P], F32)
+            nc.gpsimd.tensor_tensor(out=blend[:], in0=step_sb[:], in1=h_sb[:, :, cols], op=ALU.add)
             nc.sync.dma_start(
                 out=out_1.rearrange("(m p) j -> p m j", p=P)[:, :, cols], in_=angle_out[:]
             )
@@ -263,10 +268,56 @@ def tile_yarnixcellv4_pa_kernel(
             mx_passes(n_ps, N, c, 1)
             n_sb = candidate(c, r_ps, n_ps)
             if finished is not None:
-                outputs_of_block(c - 1, finished[0], finished[1])
+                outputs_of_block(c - 1, *turn_back(c - 1, *finished))
+            if c == BLOCKS - 1:
+                mx_passes(z_ps, Z, c, 0)
             mx_passes(z_ps, Z, c, 1)
-            z_sb = update(c, z_ps)
-            finished = (z_sb, n_sb)
-            if len(opened) == c + 1 and c + 1 < BLOCKS:
-                opened.append(open_block(c + 1))
-        outputs_of_block(BLOCKS - 1, finished[0], finished[1])
+            if c < BLOCKS - 1:
+                finished = (update(c, z_ps), n_sb)
+                if len(opened) == c + 1:
+                    opened.append(open_block(c + 1))
+
+        c = BLOCKS - 1
+        cols = slice(c * P, (c + 1) * P)
+        decayed = work.tile([P, ROW_TILES, P], F32)
+        nc.gpsimd.tensor_tensor(
+            out=decayed[:],
+            in0=angle_sb[:, :, cols],
+            in1=persist_all[:, cols].unsqueeze(1).to_broadcast([P, ROW_TILES, P]),
+            op=ALU.mult,
+        )
+        n_back = gate_banks.tile([P, ROW_TILES, P], F32, tag="bank")
+        for m in range(ROW_TILES):
+            nc.tensor.transpose(n_back[:, m, :], n_sb[:, m * P : (m + 1) * P], ident_f32[:])
+        diff = work.tile([P, ROW_TILES, P], F32)
+        nc.vector.tensor_tensor(out=diff[:], in0=n_back[:], in1=h_sb[:, :, cols], op=ALU.subtract)
+        for m in range(0, ROW_TILES, 2):
+            tiles = slice(m, m + 2)
+            z_sb = work.tile([P, 2 * P], F32, name="last_z")
+            nc.scalar.activation(
+                out=z_sb[:], in_=z_ps[:, m * P : (m + 2) * P], func=ACT.Sigmoid, bias=bias_of(Z, c)
+            )
+            z_back = gate_banks.tile([P, 2, P], F32, tag="bank")
+            for i in range(2):
+                nc.tensor.transpose(z_back[:, i, :], z_sb[:, i * P : (i + 1) * P], ident_f32[:])
+            step_sb = work.tile([P, 2, P], F32, name="last_step")
+            nc.vector.tensor_tensor(out=step_sb[:], in0=diff[:, tiles, :], in1=z_back[:], op=ALU.mult)
+            blend = work.tile([P, 2, P], F32, name="last_blend")
+            nc.gpsimd.tensor_tensor(
+                out=blend[:], in0=step_sb[:], in1=h_sb[:, tiles, cols], op=ALU.add
+            )
+            nc.sync.dma_start(
+                out=out_0.rearrange("(m p) j -> p m j", p=P)[:, tiles, cols], in_=blend[:]
+            )
+            angle_out = work.tile([P, 2, P], F32, name="last_angle")
+            nc.vector.scalar_tensor_tensor(
+                out=angle_out[:],
+                in0=z_back[:],
+                scalar=2.0 * math.pi,
+                in1=decayed[:, tiles, :],
+                op0=ALU.mult,
+                op1=ALU.add,
+            )
+            nc.sync.dma_start(
+                out=out_1.rearrange("(m p) j -> p m j", p=P)[:, tiles, cols], in_=angle_out[:]
+            )

@@ -47,19 +47,21 @@ def tile_yarnixcellv4_pa_kernel(
     nc = tc.nc
     with ExitStack() as ctx:
         keep = ctx.enter_context(tc.tile_pool(name="keep", bufs=1))
-        work = ctx.enter_context(tc.tile_pool(name="work", bufs=2))
-        gate_banks = ctx.enter_context(tc.psum_pool(name="gate_banks", bufs=6))
-        back_banks = ctx.enter_context(tc.psum_pool(name="back_banks", bufs=1))
+        work = ctx.enter_context(tc.tile_pool(name="work", bufs=4))
+        banks = ctx.enter_context(tc.psum_pool(name="banks", bufs=8))
 
-        w_planes = keep.tile([P, 2, PASSES, GATES * HIDDEN], U8, align_bytes=64)
+        w_planes = [
+            keep.tile([P, PASSES, GATES * HIDDEN], U8, align_bytes=64, name="w_planes%d" % a)
+            for a in range(2)
+        ]
         for a in range(2):
-            nc.vector.memset(w_planes[:, a, :, :].bitcast(I32), 0)
+            nc.vector.memset(w_planes[a][:].bitcast(I32), 0)
 
         def load_scales(a, scales):
             by_row = scales.rearrange("g (quad r) n -> r quad g n", r=4)
             for r in range(4):
                 nc.sync.dma_start(
-                    out=w_planes[r:P:32, a, :, :].bitcast(I32), in_=by_row[r].bitcast(I32)
+                    out=w_planes[a][r:P:32, :, :].bitcast(I32), in_=by_row[r].bitcast(I32)
                 )
 
         chunk_bytes = 2 * CHUNK_BLOCKS * P
@@ -85,14 +87,14 @@ def tile_yarnixcellv4_pa_kernel(
         h_sb = keep.tile([P, ROW_TILES, K], BF16)
         angle_sb = keep.tile([P, ROW_TILES, HIDDEN], BF16)
 
-        def load_rows(sb, dram):
+        def load_rows(sb, dram, edges):
             rows = dram.rearrange("(m p) k -> p m k", p=P)
-            for m in range(0, ROW_TILES, 2):
-                nc.sync.dma_start(out=sb[:, m : m + 2, :], in_=rows[:, m : m + 2, :])
+            for m0, m1 in zip(edges, edges[1:]):
+                nc.sync.dma_start(out=sb[:, m0:m1, :], in_=rows[:, m0:m1, :])
 
-        load_rows(x_sb, x)
+        load_rows(x_sb, x, (0, 1, 2, 4))
         load_scales(0, weight_ih_scales)
-        load_rows(h_sb, h_state)
+        load_rows(h_sb, h_state, (0, 2, 4))
         load_words(0, 0, weight_ih_words)
         load_scales(1, weight_hh_scales)
         load_words(0, 1, weight_hh_words)
@@ -135,7 +137,7 @@ def tile_yarnixcellv4_pa_kernel(
             grouped_words = grouped[:].bitcast(F32).rearrange("p g (b u) -> p g b u", u=2)
             for m in range(0, ROW_TILES, 2):
                 for g in range(PASSES):
-                    flipped = gate_banks.tile([P, 2, 2, P], F32, tag="bank")
+                    flipped = banks.tile([P, 2, 2, P], F32, tag="bank")
                     for i in range(2):
                         row_words = sb[:, m + i, :].bitcast(F32)
                         for u in range(2):
@@ -156,7 +158,7 @@ def tile_yarnixcellv4_pa_kernel(
                     in_=grouped[:, g, :],
                 )
 
-        bias_flipped = gate_banks.tile([P, P], BF16, tag="bank")
+        bias_flipped = banks.tile([P, P], BF16, tag="bank")
         nc.tensor.transpose(bias_flipped[:], bias_rows[:], ident_bf16[:])
         bias_col = keep.tile([P, GATES * BLOCKS], F32)
         nc.vector.tensor_copy(out=bias_col[:], in_=bias_flipped[:, 0 : GATES * BLOCKS])
@@ -164,7 +166,7 @@ def tile_yarnixcellv4_pa_kernel(
         persist_all = keep.tile([P, HIDDEN], BF16)
         for s in range(HIDDEN // BATCH):
             cols = slice(s * BATCH, (s + 1) * BATCH)
-            spread = gate_banks.tile([P, BATCH], F32, tag="bank")
+            spread = banks.tile([P, BATCH], F32, tag="bank")
             nc.tensor.matmul(
                 out=spread[:], lhsT=ones_bf16[:], rhs=persist_row[:, cols], start=True, stop=True
             )
@@ -177,7 +179,7 @@ def tile_yarnixcellv4_pa_kernel(
                 nc.tensor.matmul_mx(
                     out=bank[:],
                     lhsT=w_words[chunk][:, a, g, gate, 2 * P * i : 2 * P * (i + 1)].bitcast(FP4X4),
-                    lhsT_scale=w_planes[:, a, g, col : col + P],
+                    lhsT_scale=w_planes[a][:, g, col : col + P],
                     rhs=act_codes[:, a, g, :].bitcast(FP8X4),
                     rhs_scale=act_planes[:, a, g, :],
                     start=(a == 0 and g == 0),
@@ -185,13 +187,12 @@ def tile_yarnixcellv4_pa_kernel(
                 )
 
         def open_block(c):
-            r_ps = gate_banks.tile([P, BATCH], F32, tag="bank")
-            n_ps = gate_banks.tile([P, BATCH], F32, tag="bank")
-            z_ps = gate_banks.tile([P, BATCH], F32, tag="bank")
+            r_ps = banks.tile([P, BATCH], F32, tag="bank")
+            n_ps = banks.tile([P, BATCH], F32, tag="bank")
+            z_ps = banks.tile([P, BATCH], F32, tag="bank")
             mx_passes(r_ps, R, c, 0)
             mx_passes(n_ps, N, c, 0)
-            if c < BLOCKS - 1:
-                mx_passes(z_ps, Z, c, 0)
+            mx_passes(z_ps, Z, c, 0)
             return r_ps, n_ps, z_ps
 
         def bias_of(gate, c):
@@ -227,8 +228,8 @@ def tile_yarnixcellv4_pa_kernel(
                 in1=persist_all[:, cols].unsqueeze(1).to_broadcast([P, ROW_TILES, P]),
                 op=ALU.mult,
             )
-            n_back = back_banks.tile([P, ROW_TILES, P], F32)
-            z_back = back_banks.tile([P, ROW_TILES, P], F32)
+            n_back = banks.tile([P, ROW_TILES, P], F32, tag="bank")
+            z_back = banks.tile([P, ROW_TILES, P], F32, tag="bank")
             for src, back in ((n_sb, n_back), (z_sb, z_back)):
                 for m in range(ROW_TILES):
                     nc.tensor.transpose(back[:, m, :], src[:, m * P : (m + 1) * P], ident_f32[:])
@@ -261,21 +262,30 @@ def tile_yarnixcellv4_pa_kernel(
             )
 
         opened = [open_block(0), open_block(1)]
-        finished = None
+        turned_beside = {2: (0, 1), 4: (2, 3), 6: (4, 5), 7: (6,)}
+        finished = {}
         for c in range(BLOCKS):
-            r_ps, n_ps, z_ps = opened[c]
+            last = c == BLOCKS - 1
+            if c < len(opened):
+                r_ps, n_ps, z_ps = opened[c]
+            else:
+                r_ps = banks.tile([P, BATCH], F32, tag="bank")
+                mx_passes(r_ps, R, c, 0)
             mx_passes(r_ps, R, c, 1)
+            if c >= len(opened):
+                n_ps = banks.tile([P, BATCH], F32, tag="bank")
+                mx_passes(n_ps, N, c, 0)
             mx_passes(n_ps, N, c, 1)
             n_sb = candidate(c, r_ps, n_ps)
-            if finished is not None:
-                outputs_of_block(c - 1, *turn_back(c - 1, *finished))
-            if c == BLOCKS - 1:
+            turned = [(b, turn_back(b, *finished[b])) for b in turned_beside.get(c, ())]
+            for b, backs in turned:
+                outputs_of_block(b, *backs)
+            if c >= len(opened):
+                z_ps = banks.tile([P, BATCH], F32, tag="bank")
                 mx_passes(z_ps, Z, c, 0)
             mx_passes(z_ps, Z, c, 1)
-            if c < BLOCKS - 1:
-                finished = (update(c, z_ps), n_sb)
-                if len(opened) == c + 1:
-                    opened.append(open_block(c + 1))
+            if not last:
+                finished[c] = (update(c, z_ps), n_sb)
 
         c = BLOCKS - 1
         cols = slice(c * P, (c + 1) * P)
@@ -286,7 +296,7 @@ def tile_yarnixcellv4_pa_kernel(
             in1=persist_all[:, cols].unsqueeze(1).to_broadcast([P, ROW_TILES, P]),
             op=ALU.mult,
         )
-        n_back = gate_banks.tile([P, ROW_TILES, P], F32, tag="bank")
+        n_back = banks.tile([P, ROW_TILES, P], F32, tag="bank")
         for m in range(ROW_TILES):
             nc.tensor.transpose(n_back[:, m, :], n_sb[:, m * P : (m + 1) * P], ident_f32[:])
         diff = work.tile([P, ROW_TILES, P], F32)
@@ -297,13 +307,14 @@ def tile_yarnixcellv4_pa_kernel(
             nc.scalar.activation(
                 out=z_sb[:], in_=z_ps[:, m * P : (m + 2) * P], func=ACT.Sigmoid, bias=bias_of(Z, c)
             )
-            z_back = gate_banks.tile([P, 2, P], F32, tag="bank")
+            z_back = banks.tile([P, 2, P], F32, tag="bank")
             for i in range(2):
                 nc.tensor.transpose(z_back[:, i, :], z_sb[:, i * P : (i + 1) * P], ident_f32[:])
             step_sb = work.tile([P, 2, P], F32, name="last_step")
             nc.vector.tensor_tensor(out=step_sb[:], in0=diff[:, tiles, :], in1=z_back[:], op=ALU.mult)
             blend = work.tile([P, 2, P], F32, name="last_blend")
-            nc.gpsimd.tensor_tensor(
+            adder = nc.vector if m else nc.gpsimd
+            adder.tensor_tensor(
                 out=blend[:], in0=step_sb[:], in1=h_sb[:, tiles, cols], op=ALU.add
             )
             nc.sync.dma_start(

import math
from contextlib import ExitStack

import concourse.mybir as mybir
from concourse.masks import make_identity

F32 = mybir.dt.float32
BF16 = mybir.dt.bfloat16
I32 = mybir.dt.int32
U32 = mybir.dt.uint32
U8 = mybir.dt.uint8
FP8X4 = mybir.dt.float8_e4m3fn_x4
FP4X4 = mybir.dt.float4_e2m1fn_x4
ACT = mybir.ActivationFunctionType
ALU = mybir.AluOpType

P = 128
BATCH = 512
K = 1024
HIDDEN = 1024
GATES = 3
R, Z, N = 0, 1, 2
K_PASS = 4 * P
PASSES = K // K_PASS
ROW_TILES = BATCH // P
BLOCKS = HIDDEN // P
W_CHUNKS = 4
CHUNK_BLOCKS = BLOCKS // W_CHUNKS

FLOPS = 2 * BATCH * (2 * K) * (GATES * HIDDEN)


def tile_yarnixcellv4_pa_kernel(
    tc,
    x,
    h_state,
    local_angle,
    persistence,
    weight_ih_words,
    weight_ih_scales,
    weight_hh_words,
    weight_hh_scales,
    bias,
    out_0,
    out_1,
):
    nc = tc.nc
    with ExitStack() as ctx:
        keep = ctx.enter_context(tc.tile_pool(name="keep", bufs=1))
        work = ctx.enter_context(tc.tile_pool(name="work", bufs=4))
        banks = ctx.enter_context(tc.psum_pool(name="banks", bufs=8))

        w_planes = [
            keep.tile([P, PASSES, GATES * HIDDEN], U8, align_bytes=64, name="w_planes%d" % a)
            for a in range(2)
        ]
        for a in range(2):
            nc.vector.memset(w_planes[a][:].bitcast(I32), 0)

        def load_scales(a, scales):
            by_row = scales.rearrange("g (quad r) n -> r quad g n", r=4)
            for r in range(4):
                nc.sync.dma_start(
                    out=w_planes[a][r:P:32, :, :].bitcast(I32), in_=by_row[r].bitcast(I32)
                )

        chunk_bytes = 2 * CHUNK_BLOCKS * P
        w_words = [
            keep.tile(
                [P, 2, PASSES, GATES, chunk_bytes], U8, align_bytes=64, name="w_words%d" % chunk
            )
            for chunk in range(W_CHUNKS)
        ]

        def load_words(chunk, a, words):
            for g in range(PASSES):
                nc.sync.dma_start(
                    out=w_words[chunk][:, a, g, :, :].bitcast(I32),
                    in_=words[g]
                    .bitcast(I32)
                    .rearrange("p (gate q c) -> p gate q c", gate=GATES, q=W_CHUNKS)[
                        :, :, chunk, :
                    ],
                )

        x_sb = keep.tile([P, ROW_TILES, K], BF16)
        h_sb = keep.tile([P, ROW_TILES, K], BF16)
        angle_sb = keep.tile([P, ROW_TILES, HIDDEN], BF16)

        def load_rows(sb, dram, edges):
            rows = dram.rearrange("(m p) k -> p m k", p=P)
            for m0, m1 in zip(edges, edges[1:]):
                nc.sync.dma_start(out=sb[:, m0:m1, :], in_=rows[:, m0:m1, :])

        load_rows(x_sb, x, (0, 1, 2, 4))
        load_scales(0, weight_ih_scales)
        load_rows(h_sb, h_state, (0, 2, 4))
        load_words(0, 0, weight_ih_words)
        load_scales(1, weight_hh_scales)
        load_words(0, 1, weight_hh_words)
        for chunk in range(1, W_CHUNKS):
            load_words(chunk, 0, weight_ih_words)
            load_words(chunk, 1, weight_hh_words)
            if chunk == 1:
                nc.sync.dma_start(
                    out=angle_sb[:], in_=local_angle.rearrange("(m p) j -> p m j", p=P)
                )

        ident_f32 = keep.tile([P, P], F32)
        make_identity(nc, ident_f32[:])
        ident_bf16 = keep.tile([P, P], BF16)
        make_identity(nc, ident_bf16[:])
        ones_bf16 = keep.tile([P, P], BF16)
        nc.vector.memset(ones_bf16[:], 1.0)

        warm = keep.tile([P, 1], F32)
        nc.vector.memset(warm[:], 0.0)
        nc.scalar.activation(out=warm[:], in_=warm[:], func=ACT.Sigmoid)

        bias_rows = keep.tile([P, P], BF16)
        nc.vector.memset(bias_rows[:], 0.0)
        nc.gpsimd.dma_start(
            out=bias_rows[0 : GATES * BLOCKS, :], in_=bias.rearrange("(i c) -> i c", c=P)
        )
        persist_row = keep.tile([P, HIDDEN], BF16)
        nc.vector.memset(persist_row[:], 0.0)
        nc.gpsimd.dma_start(
            out=persist_row[0:1, :], in_=persistence.rearrange("(o n) -> o n", o=1)
        )

        act_codes = keep.tile([P, 2, PASSES, BATCH], U32, align_bytes=64)
        act_planes = keep.tile([P, 2, PASSES, BATCH], U8, align_bytes=64)
        for a, sb in enumerate((x_sb, h_sb)):
            grouped = keep.tile(
                [P, PASSES, 4 * BATCH], BF16, align_bytes=64, name="grouped%d" % a
            )
            grouped_words = grouped[:].bitcast(F32).rearrange("p g (b u) -> p g b u", u=2)
            for m in range(0, ROW_TILES, 2):
                for g in range(PASSES):
                    flipped = banks.tile([P, 2, 2, P], F32, tag="bank")
                    for i in range(2):
                        row_words = sb[:, m + i, :].bitcast(F32)
                        for u in range(2):
                            nc.tensor.transpose(
                                flipped[:, u, i, :],
                                row_words[:, 256 * g + u : 256 * (g + 1) : 2],
                                ident_f32[:],
                            )
                    copy_out = nc.vector.tensor_copy if g == 0 else nc.scalar.copy
                    copy_out(
                        out=grouped_words[:, g, m * P : (m + 2) * P, :],
                        in_=flipped[:].rearrange("p u i b -> p (i b) u"),
                    )
            for g in range(PASSES):
                nc.vector.quantize_mx(
                    out=act_codes[:, a, g, :].bitcast(FP8X4),
                    scales=act_planes[:, a, g, :],
                    in_=grouped[:, g, :],
                )

        bias_flipped = banks.tile([P, P], BF16, tag="bank")
        nc.tensor.transpose(bias_flipped[:], bias_rows[:], ident_bf16[:])
        bias_col = keep.tile([P, GATES * BLOCKS], F32)
        nc.vector.tensor_copy(out=bias_col[:], in_=bias_flipped[:, 0 : GATES * BLOCKS])

        persist_all = keep.tile([P, HIDDEN], BF16)
        for s in range(HIDDEN // BATCH):
            cols = slice(s * BATCH, (s + 1) * BATCH)
            spread = banks.tile([P, BATCH], F32, tag="bank")
            nc.tensor.matmul(
                out=spread[:], lhsT=ones_bf16[:], rhs=persist_row[:, cols], start=True, stop=True
            )
            nc.scalar.copy(out=persist_all[:, cols], in_=spread[:])

        def mx_passes(bank, gate, c, a):
            chunk, i = divmod(c, CHUNK_BLOCKS)
            col = gate * HIDDEN + c * P
            for g in range(PASSES):
                nc.tensor.matmul_mx(
                    out=bank[:],
                    lhsT=w_words[chunk][:, a, g, gate, 2 * P * i : 2 * P * (i + 1)].bitcast(FP4X4),
                    lhsT_scale=w_planes[a][:, g, col : col + P],
                    rhs=act_codes[:, a, g, :].bitcast(FP8X4),
                    rhs_scale=act_planes[:, a, g, :],
                    start=(a == 0 and g == 0),
                    stop=(a == 1 and g == PASSES - 1),
                )

        def open_block(c):
            r_ps = banks.tile([P, BATCH], F32, tag="bank")
            n_ps = banks.tile([P, BATCH], F32, tag="bank")
            z_ps = banks.tile([P, BATCH], F32, tag="bank")
            mx_passes(r_ps, R, c, 0)
            mx_passes(n_ps, N, c, 0)
            mx_passes(z_ps, Z, c, 0)
            return r_ps, n_ps, z_ps

        def bias_of(gate, c):
            return bias_col[:, gate * BLOCKS + c : gate * BLOCKS + c + 1]

        def candidate(c, r_ps, n_ps):
            r_sb = work.tile([P, BATCH], F32)
            nc.scalar.activation(out=r_sb[:], in_=r_ps[:], func=ACT.Sigmoid, bias=bias_of(R, c))
            rn_sb = work.tile([P, BATCH], F32)
            nc.vector.scalar_tensor_tensor(
                out=rn_sb[:],
                in0=n_ps[:],
                scalar=bias_of(N, c),
                in1=r_sb[:],
                op0=ALU.add,
                op1=ALU.mult,
            )
            n_sb = work.tile([P, BATCH], F32)
            nc.scalar.activation(out=n_sb[:], in_=rn_sb[:], func=ACT.Tanh)
            return n_sb

        def update(c, z_ps):
            z_sb = work.tile([P, BATCH], F32)
            nc.scalar.activation(out=z_sb[:], in_=z_ps[:], func=ACT.Sigmoid, bias=bias_of(Z, c))
            return z_sb

        def turn_back(c, z_sb, n_sb):
            cols = slice(c * P, (c + 1) * P)
            decayed = work.tile([P, ROW_TILES, P], F32)
            nc.gpsimd.tensor_tensor(
                out=decayed[:],
                in0=angle_sb[:, :, cols],
                in1=persist_all[:, cols].unsqueeze(1).to_broadcast([P, ROW_TILES, P]),
                op=ALU.mult,
            )
            n_back = banks.tile([P, ROW_TILES, P], F32, tag="bank")
            z_back = banks.tile([P, ROW_TILES, P], F32, tag="bank")
            for src, back in ((n_sb, n_back), (z_sb, z_back)):
                for m in range(ROW_TILES):
                    nc.tensor.transpose(back[:, m, :], src[:, m * P : (m + 1) * P], ident_f32[:])
            return decayed, n_back, z_back

        def outputs_of_block(c, decayed, n_back, z_back):
            cols = slice(c * P, (c + 1) * P)
            diff = work.tile([P, ROW_TILES, P], F32)
            nc.vector.tensor_tensor(
                out=diff[:], in0=n_back[:], in1=h_sb[:, :, cols], op=ALU.subtract
            )
            angle_out = work.tile([P, ROW_TILES, P], F32)
            nc.vector.scalar_tensor_tensor(
                out=angle_out[:],
                in0=z_back[:],
                scalar=2.0 * math.pi,
                in1=decayed[:],
                op0=ALU.mult,
                op1=ALU.add,
            )
            step_sb = work.tile([P, ROW_TILES, P], F32)
            nc.vector.tensor_tensor(out=step_sb[:], in0=diff[:], in1=z_back[:], op=ALU.mult)
            blend = work.tile([P, ROW_TILES, P], F32)
            nc.gpsimd.tensor_tensor(out=blend[:], in0=step_sb[:], in1=h_sb[:, :, cols], op=ALU.add)
            nc.sync.dma_start(
                out=out_1.rearrange("(m p) j -> p m j", p=P)[:, :, cols], in_=angle_out[:]
            )
            nc.sync.dma_start(
                out=out_0.rearrange("(m p) j -> p m j", p=P)[:, :, cols], in_=blend[:]
            )

        opened = [open_block(0), open_block(1)]
        turned_beside = {2: (0, 1), 4: (2, 3), 6: (4, 5), 7: (6,)}
        finished = {}
        for c in range(BLOCKS):
            last = c == BLOCKS - 1
            if c < len(opened):
                r_ps, n_ps, z_ps = opened[c]
            else:
                r_ps = banks.tile([P, BATCH], F32, tag="bank")
                mx_passes(r_ps, R, c, 0)
            mx_passes(r_ps, R, c, 1)
            if c >= len(opened):
                n_ps = banks.tile([P, BATCH], F32, tag="bank")
                mx_passes(n_ps, N, c, 0)
            mx_passes(n_ps, N, c, 1)
            n_sb = candidate(c, r_ps, n_ps)
            turned = [(b, turn_back(b, *finished[b])) for b in turned_beside.get(c, ())]
            for b, backs in turned:
                outputs_of_block(b, *backs)
            if c >= len(opened):
                z_ps = banks.tile([P, BATCH], F32, tag="bank")
                mx_passes(z_ps, Z, c, 0)
            mx_passes(z_ps, Z, c, 1)
            if not last:
                finished[c] = (update(c, z_ps), n_sb)

        c = BLOCKS - 1
        cols = slice(c * P, (c + 1) * P)
        decayed = work.tile([P, ROW_TILES, P], F32)
        nc.gpsimd.tensor_tensor(
            out=decayed[:],
            in0=angle_sb[:, :, cols],
            in1=persist_all[:, cols].unsqueeze(1).to_broadcast([P, ROW_TILES, P]),
            op=ALU.mult,
        )
        n_back = banks.tile([P, ROW_TILES, P], F32, tag="bank")
        for m in range(ROW_TILES):
            nc.tensor.transpose(n_back[:, m, :], n_sb[:, m * P : (m + 1) * P], ident_f32[:])
        diff = work.tile([P, ROW_TILES, P], F32)
        nc.vector.tensor_tensor(out=diff[:], in0=n_back[:], in1=h_sb[:, :, cols], op=ALU.subtract)
        for m in range(0, ROW_TILES, 2):
            tiles = slice(m, m + 2)
            z_sb = work.tile([P, 2 * P], F32, name="last_z")
            nc.scalar.activation(
                out=z_sb[:], in_=z_ps[:, m * P : (m + 2) * P], func=ACT.Sigmoid, bias=bias_of(Z, c)
            )
            z_back = banks.tile([P, 2, P], F32, tag="bank")
            for i in range(2):
                nc.tensor.transpose(z_back[:, i, :], z_sb[:, i * P : (i + 1) * P], ident_f32[:])
            step_sb = work.tile([P, 2, P], F32, name="last_step")
            nc.vector.tensor_tensor(out=step_sb[:], in0=diff[:, tiles, :], in1=z_back[:], op=ALU.mult)
            blend = work.tile([P, 2, P], F32, name="last_blend")
            adder = nc.vector if m else nc.gpsimd
            adder.tensor_tensor(
                out=blend[:], in0=step_sb[:], in1=h_sb[:, tiles, cols], op=ALU.add
            )
            nc.sync.dma_start(
                out=out_0.rearrange("(m p) j -> p m j", p=P)[:, tiles, cols], in_=blend[:]
            )
            angle_out = work.tile([P, 2, P], F32, name="last_angle")
            nc.vector.scalar_tensor_tensor(
                out=angle_out[:],
                in0=z_back[:],
                scalar=2.0 * math.pi,
                in1=decayed[:, tiles, :],
                op0=ALU.mult,
                op1=ALU.add,
            )
            nc.sync.dma_start(
                out=out_1.rearrange("(m p) j -> p m j", p=P)[:, tiles, cols], in_=angle_out[:]
            )
